import numpy as np
import ml_dtypes


def mxq(x, axis, fmt="e4m3"):
    dtype, down = {"e4m3": (ml_dtypes.float8_e4m3fn, 7), "e5m2": (ml_dtypes.float8_e5m2, 14)}[fmt]
    v = np.moveaxis(np.asarray(x, np.float32).astype(ml_dtypes.bfloat16).astype(np.float64), axis, -1)
    blocks = v.reshape(v.shape[:-1] + (-1, 32))
    amax = np.abs(blocks).max(-1, keepdims=True)
    byte = np.maximum(np.where(amax > 0, np.frexp(amax)[1] - 1 + 127, 0) - down, 1)
    scale = np.exp2(byte - 127.0)
    codes = (blocks / scale).astype(np.float32).astype(dtype).astype(np.float64)
    return np.moveaxis((codes * scale).reshape(v.shape), -1, axis)


WIDE = False


def mx_kscale(k):
    if not WIDE:
        return np.ones(k)
    levels = np.array([10, -10, 5, -5, 0])
    a = np.random.permutation(np.resize(levels, k // 512 * 4)).reshape(k // 512, 4)
    idx = np.arange(k)
    return np.exp2(a[idx // 512, idx % 128 // 32])


BF16 = ml_dtypes.bfloat16


def bf(x):
    return np.asarray(x, np.float32).astype(BF16)


def f64(x):
    return np.asarray(x).astype(np.float64)


E2M1 = np.array([0.0, 0.5, 1.0, 1.5, 2.0, 3.0, 4.0, 6.0, -0.0, -0.5, -1.0, -1.5, -2.0, -3.0, -4.0, -6.0])


def pack_weight(w, fmt):
    k, n = w.shape
    w = f64(bf(w)).reshape(k // 32, 32, n)
    amax = np.abs(w).max(1)
    if fmt == "e4m3":
        byte = np.frexp(amax)[1] - 1 + 127 - 7
    else:
        mant, ex = np.frexp(amax / 6.0)
        byte = np.where(mant > 0.5, ex, ex - 1) + 127
    byte = np.clip(np.where(amax > 0, byte, 1), 1, 254)
    scaled = (w * np.exp2(127.0 - byte)[:, None, :]).reshape(k, n).astype(np.float32)
    by_word = np.ascontiguousarray(scaled.reshape(k // 512, 128, 4, n).transpose(0, 1, 3, 2))
    if fmt == "e4m3":
        words = by_word.astype(ml_dtypes.float8_e4m3fn).view(np.uint8)
    else:
        c = by_word.astype(ml_dtypes.float4_e2m1fn).view(np.uint8) & 0xF
        words = c[..., 0::2] | (c[..., 1::2] << 4)
    return np.ascontiguousarray(words), np.ascontiguousarray(byte.astype(np.uint8).reshape(k // 512, 16, n))


def unpack_weight(words, scales, fmt):
    g, p, n, _ = words.shape
    if fmt == "e4m3":
        vals = np.ascontiguousarray(words).view(ml_dtypes.float8_e4m3fn).astype(np.float64)
    else:
        nib = np.empty((g, p, n, 4), np.uint8)
        nib[..., 0::2] = words & 0xF
        nib[..., 1::2] = words >> 4
        vals = E2M1[nib]
    vals = vals * np.repeat(np.exp2(scales.astype(np.float64) - 127.0), 8, axis=1)[..., None]
    return vals.transpose(0, 1, 3, 2).reshape(g * 512, n)


M, SP, H, FF, NH = 4096, 3072, 512, 2560, 8
EPS = 1.1920929e-07
G = 2


def rms_norm(x, w):
    var = np.mean(np.square(x), axis=-1, keepdims=True)
    return x * (1.0 / np.sqrt(var + EPS)) * w


def setup_inputs():
    s = mx_kscale(H)
    x = bf(np.random.standard_normal((M, H)))
    stack = np.random.standard_normal((G, H, 3 * H)) * 1.25 / np.sqrt(H) / s[None, :, None]
    words, scales = pack_weight(stack.reshape(-1, 3 * H), "e4m3")
    ln1 = bf((1.0 + 0.1 * np.random.standard_normal((2, H))) * s)
    return {"x": x, "W_qkv_words": words, "W_qkv_scales": scales, "ln1": ln1}


def reference(x, W_qkv_words, W_qkv_scales, ln1):
    x, ln1 = f64(x), f64(ln1)
    W_qkv = unpack_weight(W_qkv_words, W_qkv_scales, "e4m3").reshape(G, H, 3 * H)
    h0 = rms_norm(x[:SP], ln1[0])
    h1 = rms_norm(x[SP:], ln1[1])
    y0 = mxq(h0, 1, "e4m3") @ W_qkv[0]
    y1 = mxq(h1, 1, "e4m3") @ W_qkv[1]
    return np.concatenate([y0, y1], axis=0)

@@ -1,0 +1,190 @@
+from contextlib import ExitStack
+
+import concourse.mybir as mybir
+from concourse.masks import make_identity
+
+F32 = mybir.dt.float32
+BF16 = mybir.dt.bfloat16
+I32 = mybir.dt.int32
+U32 = mybir.dt.uint32
+U8 = mybir.dt.uint8
+FP8X4 = mybir.dt.float8_e4m3fn_x4
+ACT = mybir.ActivationFunctionType
+ALU = mybir.AluOpType
+
+P = 128
+PACK = 4
+ROWS = 4096
+MODEL_1_FIRST_ROW = 3072
+H = 512
+N_OUT = 1536
+MODELS = 2
+EPS = 1.1920929e-07
+
+BANK_COLS = 512
+BANKS_PER_TILE = N_OUT // BANK_COLS
+GROUP_TILES = 4
+GROUP_ROWS = GROUP_TILES * P
+GROUPS = ROWS // GROUP_ROWS
+PAIR = 2
+PAIRS_PER_GROUP = GROUP_TILES // PAIR
+PAIRS = GROUPS * PAIRS_PER_GROUP
+PAIR_BANKS = PAIR * BANKS_PER_TILE
+SCALAR_BANKS = 4
+SCALE_ROWS_PER_QUADRANT = 4
+QUADRANTS = 4
+
+FLOPS = 2 * ROWS * H * N_OUT
+
+
+def tile_twomodelblockrouted_pa_t_e_kernel(tc, x, W_qkv_words, W_qkv_scales, ln1, out):
+    nc = tc.nc
+    x_groups = x.rearrange("(g p j) k -> g p j k", p=P, j=GROUP_TILES)
+    out_groups = out.rearrange("(g p j) n -> g p j n", p=P, j=GROUP_TILES)
+
+    with ExitStack() as ctx:
+        ctx.enter_context(tc.manual_schedule())
+        const = ctx.enter_context(tc.tile_pool(name="const", bufs=1))
+        x_pool = ctx.enter_context(tc.tile_pool(name="x", bufs=GROUPS))
+        scratch = ctx.enter_context(tc.tile_pool(name="scratch", bufs=4))
+        small = ctx.enter_context(tc.tile_pool(name="small", bufs=3))
+        y_pool = ctx.enter_context(tc.tile_pool(name="y", bufs=3))
+        h_pool = ctx.enter_context(tc.tile_pool(name="h", bufs=2))
+        out_pool = ctx.enter_context(tc.tile_pool(name="out", bufs=8))
+        psum_t = ctx.enter_context(tc.psum_pool(name="psum_t", bufs=PAIR))
+        psum_o = ctx.enter_context(tc.psum_pool(name="psum_o", bufs=PAIR_BANKS))
+
+        w_planes = const.tile([P, MODELS, N_OUT], U8, align_bytes=64)
+        nc.vector.memset(w_planes[:].bitcast(I32), 0)
+        eps = const.tile([P, 1], F32)
+        nc.vector.memset(eps[:], EPS)
+        ident = const.tile([P, P], F32)
+        make_identity(nc, ident[:])
+        table_warmer = const.tile([P, 1], F32)
+        nc.scalar.activation(out=table_warmer[:], in_=eps[:], func=ACT.Sqrt)
+
+        x_tiles = []
+        for g in range(GROUPS):
+            x_g = x_pool.tile([P, GROUP_TILES, H], BF16)
+            x_tiles.append(x_g)
+        w_words = const.tile([P, MODELS, N_OUT], U32, align_bytes=64)
+        gain = const.tile([P, MODELS, PACK], BF16)
+
+        def load_x(g):
+            nc.sync.dma_start(out=x_tiles[g][:], in_=x_groups[g])
+
+        def load_w_words(e):
+            nc.sync.dma_start(
+                out=w_words[:, e, :].bitcast(I32),
+                in_=W_qkv_words[e].rearrange("p n t -> p (n t)").bitcast(I32),
+            )
+
+        load_x(0)
+        nc.sync.dma_start(out=gain[:], in_=ln1.rearrange("e (p t) -> p e t", t=PACK))
+        for quadrant in range(QUADRANTS):
+            first = quadrant * SCALE_ROWS_PER_QUADRANT
+            nc.sync.dma_start(
+                out=w_planes[32 * quadrant : 32 * quadrant + SCALE_ROWS_PER_QUADRANT, :, :].bitcast(I32),
+                in_=W_qkv_scales[:, first : first + SCALE_ROWS_PER_QUADRANT, :]
+                .rearrange("e q n -> q e n")
+                .bitcast(I32),
+            )
+        load_w_words(0)
+        for g in range(1, GROUPS):
+            load_x(g)
+        load_w_words(1)
+
+        std_of = {}
+        y_of = {}
+        h_of = {}
+        mx_of = {}
+
+        def x_tile(i, jj):
+            g, half = divmod(i, PAIRS_PER_GROUP)
+            return x_tiles[g][:, half * PAIR + jj, :]
+
+        def model_of(i):
+            return 0 if i * PAIR * P < MODEL_1_FIRST_ROW else 1
+
+        def stats(i):
+            sum_sq = small.tile([P, PAIR], F32)
+            for jj in range(PAIR):
+                squares = scratch.tile([P, H], BF16)
+                nc.scalar.activation(
+                    out=squares[:], in_=x_tile(i, jj), func=ACT.Square, accum_out=sum_sq[:, jj : jj + 1]
+                )
+            std = small.tile([P, PAIR], F32)
+            nc.scalar.activation(out=std[:], in_=sum_sq[:], func=ACT.Sqrt, scale=1.0 / H, bias=eps[:, 0:1])
+            std_of[i] = std
+
+        def scale(i):
+            rstd = small.tile([P, PAIR], F32)
+            nc.vector.reciprocal(out=rstd[:], in_=std_of[i][:])
+            y = y_pool.tile([P, PAIR, PACK, P], F32)
+            for jj in range(PAIR):
+                nc.vector.tensor_scalar_mul(
+                    out=y[:, jj, :, :],
+                    in0=x_tile(i, jj).rearrange("p (c t) -> p t c", t=PACK),
+                    scalar1=rstd[:, jj : jj + 1],
+                )
+            y_of[i] = y
+
+        def transpose(i):
+            h = h_pool.tile([P, PAIR, P, PACK], BF16, align_bytes=64)
+            for jj in range(PAIR):
+                yT = psum_t.tile([P, PACK, P], F32)
+                for t in range(PACK):
+                    nc.tensor.transpose(yT[:, t, :], y_of[i][:, jj, t, :], ident[:])
+                nc.vector.tensor_tensor(
+                    out=h[:, jj, :, :],
+                    in0=yT[:].rearrange("p t r -> p r t"),
+                    in1=gain[:, model_of(i), :].unsqueeze(1).to_broadcast([P, P, PACK]),
+                    op=ALU.mult,
+                )
+            h_of[i] = h
+
+        def quantise(i):
+            h_words = h_pool.tile([P, PAIR * P], U32, align_bytes=64)
+            h_planes = h_pool.tile([P, PAIR * P], U8, align_bytes=64)
+            nc.vector.quantize_mx(
+                out=h_words[:].bitcast(FP8X4),
+                scales=h_planes[:],
+                in_=h_of[i][:].rearrange("p j r t -> p (j r t)"),
+            )
+            mx_of[i] = (h_words, h_planes)
+
+        def multiply(i):
+            e = model_of(i)
+            h_words, h_planes = mx_of[i]
+            result = out_pool.tile([P, PAIR, N_OUT], F32)
+            for bank in range(PAIR_BANKS):
+                jj, block = divmod(bank, BANKS_PER_TILE)
+                rows = slice(jj * P, (jj + 1) * P)
+                cols = slice(block * BANK_COLS, (block + 1) * BANK_COLS)
+                acc = psum_o.tile([P, BANK_COLS], F32)
+                nc.tensor.matmul_mx(
+                    out=acc[:],
+                    lhsT=h_words[:, rows].bitcast(FP8X4),
+                    lhsT_scale=h_planes[:, rows],
+                    rhs=w_words[:, e, cols].bitcast(FP8X4),
+                    rhs_scale=w_planes[:, e, cols],
+                    start=True,
+                    stop=True,
+                )
+                if bank < SCALAR_BANKS:
+                    nc.scalar.copy(out=result[:, jj, cols], in_=acc[:])
+                else:
+                    nc.vector.tensor_copy(out=result[:, jj, cols], in_=acc[:])
+            g, half = divmod(i, PAIRS_PER_GROUP)
+            nc.sync.dma_start(out=out_groups[g][:, half * PAIR : (half + 1) * PAIR, :], in_=result[:])
+
+        def run(stage, i):
+            if 0 <= i < PAIRS:
+                stage(i)
+
+        for step in range(PAIRS + 3):
+            run(quantise, step - 3)
+            run(stats, step)
+            run(scale, step - 1)
+            run(transpose, step - 2)
+            run(multiply, step - 3)

@@ -30,7 +30,6 @@ PAIR = 2
 PAIRS_PER_GROUP = GROUP_TILES // PAIR
 PAIRS = GROUPS * PAIRS_PER_GROUP
 PAIR_BANKS = PAIR * BANKS_PER_TILE
-SCALAR_BANKS = 4
 SCALE_ROWS_PER_QUADRANT = 4
 QUADRANTS = 4
 
@@ -122,10 +121,13 @@ def tile_twomodelblockrouted_pa_t_e_kernel(tc, x, W_qkv_words, W_qkv_scales, ln1
             nc.vector.reciprocal(out=rstd[:], in_=std_of[i][:])
             y = y_pool.tile([P, PAIR, PACK, P], F32)
             for jj in range(PAIR):
-                nc.vector.tensor_scalar_mul(
+                nc.gpsimd.tensor_scalar(
                     out=y[:, jj, :, :],
                     in0=x_tile(i, jj).rearrange("p (c t) -> p t c", t=PACK),
                     scalar1=rstd[:, jj : jj + 1],
+                    scalar2=1.0,
+                    op0=ALU.mult,
+                    op1=ALU.mult,
                 )
             y_of[i] = y
 
@@ -171,7 +173,7 @@ def tile_twomodelblockrouted_pa_t_e_kernel(tc, x, W_qkv_words, W_qkv_scales, ln1
                     start=True,
                     stop=True,
                 )
-                if bank < SCALAR_BANKS:
+                if bank % 2 == 0:
                     nc.scalar.copy(out=result[:, jj, cols], in_=acc[:])
                 else:
                     nc.vector.tensor_copy(out=result[:, jj, cols], in_=acc[:])

@@ -64,9 +64,9 @@ def tile_twomodelblockrouted_pa_t_e_kernel(tc, x, W_qkv_words, W_qkv_scales, ln1
 
         x_tiles = []
         for g in range(GROUPS):
-            x_g = x_pool.tile([P, GROUP_TILES, H], BF16)
+            x_g = x_pool.tile([P, GROUP_TILES, H], BF16, align_bytes=256)
             x_tiles.append(x_g)
-        w_words = const.tile([P, MODELS, N_OUT], U32, align_bytes=64)
+        w_words = const.tile([P, MODELS, N_OUT], U32, align_bytes=256)
         gain = const.tile([P, MODELS, PACK], BF16)
 
         def load_x(g):
@@ -158,7 +158,7 @@ def tile_twomodelblockrouted_pa_t_e_kernel(tc, x, W_qkv_words, W_qkv_scales, ln1
         def multiply(i):
             e = model_of(i)
             h_words, h_planes = mx_of[i]
-            result = out_pool.tile([P, PAIR, N_OUT], F32)
+            result = out_pool.tile([P, PAIR, N_OUT], F32, align_bytes=256)
             for bank in range(PAIR_BANKS):
                 jj, block = divmod(bank, BANKS_PER_TILE)
                 rows = slice(jj * P, (jj + 1) * P)

@@ -64,9 +64,9 @@ def tile_twomodelblockrouted_pa_t_e_kernel(tc, x, W_qkv_words, W_qkv_scales, ln1
 
         x_tiles = []
         for g in range(GROUPS):
-            x_g = x_pool.tile([P, GROUP_TILES, H], BF16, align_bytes=256)
+            x_g = x_pool.tile([P, GROUP_TILES, H], BF16, align_bytes=4096)
             x_tiles.append(x_g)
-        w_words = const.tile([P, MODELS, N_OUT], U32, align_bytes=256)
+        w_words = const.tile([P, MODELS, N_OUT], U32, align_bytes=4096)
         gain = const.tile([P, MODELS, PACK], BF16)
 
         def load_x(g):
@@ -158,7 +158,7 @@ def tile_twomodelblockrouted_pa_t_e_kernel(tc, x, W_qkv_words, W_qkv_scales, ln1
         def multiply(i):
             e = model_of(i)
             h_words, h_planes = mx_of[i]
-            result = out_pool.tile([P, PAIR, N_OUT], F32, align_bytes=256)
+            result = out_pool.tile([P, PAIR, N_OUT], F32, align_bytes=4096)
             for bank in range(PAIR_BANKS):
                 jj, block = divmod(bank, BANKS_PER_TILE)
                 rows = slice(jj * P, (jj + 1) * P)

@@ -31,7 +31,6 @@ PAIRS_PER_GROUP = GROUP_TILES // PAIR
 PAIRS = GROUPS * PAIRS_PER_GROUP
 PAIR_BANKS = PAIR * BANKS_PER_TILE
 SCALE_ROWS_PER_QUADRANT = 4
-QUADRANTS = 4
 
 FLOPS = 2 * ROWS * H * N_OUT
 
@@ -80,13 +79,10 @@ def tile_twomodelblockrouted_pa_t_e_kernel(tc, x, W_qkv_words, W_qkv_scales, ln1
 
         load_x(0)
         nc.sync.dma_start(out=gain[:], in_=ln1.rearrange("e (p t) -> p e t", t=PACK))
-        for quadrant in range(QUADRANTS):
-            first = quadrant * SCALE_ROWS_PER_QUADRANT
+        for r in range(SCALE_ROWS_PER_QUADRANT):
             nc.sync.dma_start(
-                out=w_planes[32 * quadrant : 32 * quadrant + SCALE_ROWS_PER_QUADRANT, :, :].bitcast(I32),
-                in_=W_qkv_scales[:, first : first + SCALE_ROWS_PER_QUADRANT, :]
-                .rearrange("e q n -> q e n")
-                .bitcast(I32),
+                out=w_planes[r : P : 32, :, :].bitcast(I32),
+                in_=W_qkv_scales[:, r : 16 : 4, :].rearrange("e q n -> q e n").bitcast(I32),
             )
         load_w_words(0)
         for g in range(1, GROUPS):

@@ -21,15 +21,15 @@ N_OUT = 1536
 MODELS = 2
 EPS = 1.1920929e-07
 
+MODEL_0_TILES = MODEL_1_FIRST_ROW // P
+TILES = ROWS // P
 BANK_COLS = 512
 BANKS_PER_TILE = N_OUT // BANK_COLS
-GROUP_TILES = 4
-GROUP_ROWS = GROUP_TILES * P
-GROUPS = ROWS // GROUP_ROWS
 PAIR = 2
-PAIRS_PER_GROUP = GROUP_TILES // PAIR
-PAIRS = GROUPS * PAIRS_PER_GROUP
-PAIR_BANKS = PAIR * BANKS_PER_TILE
+UNITS = [(0, 1), (1, 1)] + [(t, PAIR) for t in range(PAIR, TILES, PAIR)]
+X_CHUNKS_FIRST = [(0, 2), (2, 2), (4, 4)]
+X_CHUNKS_REST = [(8, 16), (24, 8)]
+OUT_BANKS = 6
 SCALE_ROWS_PER_QUADRANT = 4
 
 FLOPS = 2 * ROWS * H * N_OUT
@@ -37,20 +37,30 @@ FLOPS = 2 * ROWS * H * N_OUT
 
 def tile_twomodelblockrouted_pa_t_e_kernel(tc, x, W_qkv_words, W_qkv_scales, ln1, out):
     nc = tc.nc
-    x_groups = x.rearrange("(g p j) k -> g p j k", p=P, j=GROUP_TILES)
-    out_groups = out.rearrange("(g p j) n -> g p j n", p=P, j=GROUP_TILES)
+    x_models = (
+        x[:MODEL_1_FIRST_ROW, :].rearrange("(p j) k -> p j k", p=P),
+        x[MODEL_1_FIRST_ROW:, :].rearrange("(p j) k -> p j k", p=P),
+    )
+    out_models = (
+        out[:MODEL_1_FIRST_ROW, :].rearrange("(p j) n -> p j n", p=P),
+        out[MODEL_1_FIRST_ROW:, :].rearrange("(p j) n -> p j n", p=P),
+    )
+
+    def model_and_tiles(first, count):
+        if first < MODEL_0_TILES:
+            return 0, slice(first, first + count)
+        return 1, slice(first - MODEL_0_TILES, first - MODEL_0_TILES + count)
 
     with ExitStack() as ctx:
         ctx.enter_context(tc.manual_schedule())
         const = ctx.enter_context(tc.tile_pool(name="const", bufs=1))
-        x_pool = ctx.enter_context(tc.tile_pool(name="x", bufs=GROUPS))
         scratch = ctx.enter_context(tc.tile_pool(name="scratch", bufs=4))
         small = ctx.enter_context(tc.tile_pool(name="small", bufs=3))
         y_pool = ctx.enter_context(tc.tile_pool(name="y", bufs=3))
         h_pool = ctx.enter_context(tc.tile_pool(name="h", bufs=2))
         out_pool = ctx.enter_context(tc.tile_pool(name="out", bufs=8))
         psum_t = ctx.enter_context(tc.psum_pool(name="psum_t", bufs=PAIR))
-        psum_o = ctx.enter_context(tc.psum_pool(name="psum_o", bufs=PAIR_BANKS))
+        psum_o = ctx.enter_context(tc.psum_pool(name="psum_o", bufs=OUT_BANKS))
 
         w_planes = const.tile([P, MODELS, N_OUT], U8, align_bytes=64)
         nc.vector.memset(w_planes[:].bitcast(I32), 0)
@@ -61,15 +71,13 @@ def tile_twomodelblockrouted_pa_t_e_kernel(tc, x, W_qkv_words, W_qkv_scales, ln1
         table_warmer = const.tile([P, 1], F32)
         nc.scalar.activation(out=table_warmer[:], in_=eps[:], func=ACT.Sqrt)
 
-        x_tiles = []
-        for g in range(GROUPS):
-            x_g = x_pool.tile([P, GROUP_TILES, H], BF16, align_bytes=4096)
-            x_tiles.append(x_g)
+        x_all = const.tile([P, TILES, H], BF16, align_bytes=4096)
         w_words = const.tile([P, MODELS, N_OUT], U32, align_bytes=4096)
         gain = const.tile([P, MODELS, PACK], BF16)
 
-        def load_x(g):
-            nc.sync.dma_start(out=x_tiles[g][:], in_=x_groups[g])
+        def load_x(first, count):
+            model, tiles = model_and_tiles(first, count)
+            nc.sync.dma_start(out=x_all[:, first : first + count, :], in_=x_models[model][:, tiles, :])
 
         def load_w_words(e):
             nc.sync.dma_start(
@@ -77,49 +85,52 @@ def tile_twomodelblockrouted_pa_t_e_kernel(tc, x, W_qkv_words, W_qkv_scales, ln1
                 in_=W_qkv_words[e].rearrange("p n t -> p (n t)").bitcast(I32),
             )
 
-        load_x(0)
+        load_x(*X_CHUNKS_FIRST[0])
         nc.sync.dma_start(out=gain[:], in_=ln1.rearrange("e (p t) -> p e t", t=PACK))
         for r in range(SCALE_ROWS_PER_QUADRANT):
             nc.sync.dma_start(
                 out=w_planes[r : P : 32, :, :].bitcast(I32),
                 in_=W_qkv_scales[:, r : 16 : 4, :].rearrange("e q n -> q e n").bitcast(I32),
             )
+        for first, count in X_CHUNKS_FIRST[1:]:
+            load_x(first, count)
         load_w_words(0)
-        for g in range(1, GROUPS):
-            load_x(g)
+        for first, count in X_CHUNKS_REST:
+            load_x(first, count)
         load_w_words(1)
 
         std_of = {}
         y_of = {}
         h_of = {}
         mx_of = {}
-
-        def x_tile(i, jj):
-            g, half = divmod(i, PAIRS_PER_GROUP)
-            return x_tiles[g][:, half * PAIR + jj, :]
+        result_of = {}
 
         def model_of(i):
-            return 0 if i * PAIR * P < MODEL_1_FIRST_ROW else 1
+            return 0 if UNITS[i][0] < MODEL_0_TILES else 1
 
         def stats(i):
+            first, count = UNITS[i]
             sum_sq = small.tile([P, PAIR], F32)
-            for jj in range(PAIR):
+            for jj in range(count):
                 squares = scratch.tile([P, H], BF16)
                 nc.scalar.activation(
-                    out=squares[:], in_=x_tile(i, jj), func=ACT.Square, accum_out=sum_sq[:, jj : jj + 1]
+                    out=squares[:], in_=x_all[:, first + jj, :], func=ACT.Square, accum_out=sum_sq[:, jj : jj + 1]
                 )
             std = small.tile([P, PAIR], F32)
-            nc.scalar.activation(out=std[:], in_=sum_sq[:], func=ACT.Sqrt, scale=1.0 / H, bias=eps[:, 0:1])
+            nc.scalar.activation(
+                out=std[:, :count], in_=sum_sq[:, :count], func=ACT.Sqrt, scale=1.0 / H, bias=eps[:, 0:1]
+            )
             std_of[i] = std
 
         def scale(i):
+            first, count = UNITS[i]
             rstd = small.tile([P, PAIR], F32)
-            nc.vector.reciprocal(out=rstd[:], in_=std_of[i][:])
+            nc.vector.reciprocal(out=rstd[:, :count], in_=std_of[i][:, :count])
             y = y_pool.tile([P, PAIR, PACK, P], F32)
-            for jj in range(PAIR):
+            for jj in range(count):
                 nc.gpsimd.tensor_scalar(
                     out=y[:, jj, :, :],
-                    in0=x_tile(i, jj).rearrange("p (c t) -> p t c", t=PACK),
+                    in0=x_all[:, first + jj, :].rearrange("p (c t) -> p t c", t=PACK),
                     scalar1=rstd[:, jj : jj + 1],
                     scalar2=1.0,
                     op0=ALU.mult,
@@ -128,8 +139,9 @@ def tile_twomodelblockrouted_pa_t_e_kernel(tc, x, W_qkv_words, W_qkv_scales, ln1
             y_of[i] = y
 
         def transpose(i):
+            count = UNITS[i][1]
             h = h_pool.tile([P, PAIR, P, PACK], BF16, align_bytes=64)
-            for jj in range(PAIR):
+            for jj in range(count):
                 yT = psum_t.tile([P, PACK, P], F32)
                 for t in range(PACK):
                     nc.tensor.transpose(yT[:, t, :], y_of[i][:, jj, t, :], ident[:])
@@ -142,45 +154,52 @@ def tile_twomodelblockrouted_pa_t_e_kernel(tc, x, W_qkv_words, W_qkv_scales, ln1
             h_of[i] = h
 
         def quantise(i):
+            rows = UNITS[i][1] * P
             h_words = h_pool.tile([P, PAIR * P], U32, align_bytes=64)
             h_planes = h_pool.tile([P, PAIR * P], U8, align_bytes=64)
             nc.vector.quantize_mx(
-                out=h_words[:].bitcast(FP8X4),
-                scales=h_planes[:],
-                in_=h_of[i][:].rearrange("p j r t -> p (j r t)"),
+                out=h_words[:, :rows].bitcast(FP8X4),
+                scales=h_planes[:, :rows],
+                in_=h_of[i][:, : UNITS[i][1], :, :].rearrange("p j r t -> p (j r t)"),
             )
             mx_of[i] = (h_words, h_planes)
 
         def multiply(i):
             e = model_of(i)
             h_words, h_planes = mx_of[i]
-            result = out_pool.tile([P, PAIR, N_OUT], F32, align_bytes=4096)
-            for bank in range(PAIR_BANKS):
-                jj, block = divmod(bank, BANKS_PER_TILE)
+            first, count = UNITS[i]
+            for jj in range(count):
+                group, place = divmod(first + jj, PAIR)
+                if place == 0:
+                    result = out_pool.tile([P, PAIR, N_OUT], F32, align_bytes=4096)
+                    result_of[group] = result
                 rows = slice(jj * P, (jj + 1) * P)
-                cols = slice(block * BANK_COLS, (block + 1) * BANK_COLS)
-                acc = psum_o.tile([P, BANK_COLS], F32)
-                nc.tensor.matmul_mx(
-                    out=acc[:],
-                    lhsT=h_words[:, rows].bitcast(FP8X4),
-                    lhsT_scale=h_planes[:, rows],
-                    rhs=w_words[:, e, cols].bitcast(FP8X4),
-                    rhs_scale=w_planes[:, e, cols],
-                    start=True,
-                    stop=True,
-                )
-                if bank % 2 == 0:
-                    nc.scalar.copy(out=result[:, jj, cols], in_=acc[:])
-                else:
-                    nc.vector.tensor_copy(out=result[:, jj, cols], in_=acc[:])
-            g, half = divmod(i, PAIRS_PER_GROUP)
-            nc.sync.dma_start(out=out_groups[g][:, half * PAIR : (half + 1) * PAIR, :], in_=result[:])
+                for block in range(BANKS_PER_TILE):
+                    cols = slice(block * BANK_COLS, (block + 1) * BANK_COLS)
+                    acc = psum_o.tile([P, BANK_COLS], F32)
+                    nc.tensor.matmul_mx(
+                        out=acc[:],
+                        lhsT=h_words[:, rows].bitcast(FP8X4),
+                        lhsT_scale=h_planes[:, rows],
+                        rhs=w_words[:, e, cols].bitcast(FP8X4),
+                        rhs_scale=w_planes[:, e, cols],
+                        start=True,
+                        stop=True,
+                    )
+                    bank = (first + jj) * BANKS_PER_TILE + block
+                    if (bank % 9) % 2 == 0:
+                        nc.scalar.copy(out=result_of[group][:, place, cols], in_=acc[:])
+                    else:
+                        nc.vector.tensor_copy(out=result_of[group][:, place, cols], in_=acc[:])
+                if place == PAIR - 1:
+                    model, tiles = model_and_tiles(group * PAIR, PAIR)
+                    nc.sync.dma_start(out=out_models[model][:, tiles, :], in_=result_of[group][:])
 
         def run(stage, i):
-            if 0 <= i < PAIRS:
+            if 0 <= i < len(UNITS):
                 stage(i)
 
-        for step in range(PAIRS + 3):
+        for step in range(len(UNITS) + 3):
             run(quantise, step - 3)
             run(stats, step)
             run(scale, step - 1)

from contextlib import ExitStack

import concourse.mybir as mybir
from concourse.masks import make_identity

F32 = mybir.dt.float32
BF16 = mybir.dt.bfloat16
I32 = mybir.dt.int32
U32 = mybir.dt.uint32
U8 = mybir.dt.uint8
FP8X4 = mybir.dt.float8_e4m3fn_x4
ACT = mybir.ActivationFunctionType
ALU = mybir.AluOpType

P = 128
PACK = 4
ROWS = 4096
MODEL_1_FIRST_ROW = 3072
H = 512
N_OUT = 1536
MODELS = 2
EPS = 1.1920929e-07

MODEL_0_TILES = MODEL_1_FIRST_ROW // P
TILES = ROWS // P
BANK_COLS = 512
BANKS_PER_TILE = N_OUT // BANK_COLS
PAIR = 2
UNITS = [(0, 1), (1, 1)] + [(t, PAIR) for t in range(PAIR, TILES, PAIR)]
X_CHUNKS_FIRST = [(0, 2), (2, 2), (4, 4)]
X_CHUNKS_REST = [(8, 16), (24, 8)]
OUT_BANKS = 6
SCALE_ROWS_PER_QUADRANT = 4

FLOPS = 2 * ROWS * H * N_OUT


def tile_twomodelblockrouted_pa_t_e_kernel(tc, x, W_qkv_words, W_qkv_scales, ln1, out):
    nc = tc.nc
    x_models = (
        x[:MODEL_1_FIRST_ROW, :].rearrange("(p j) k -> p j k", p=P),
        x[MODEL_1_FIRST_ROW:, :].rearrange("(p j) k -> p j k", p=P),
    )
    out_models = (
        out[:MODEL_1_FIRST_ROW, :].rearrange("(p j) n -> p j n", p=P),
        out[MODEL_1_FIRST_ROW:, :].rearrange("(p j) n -> p j n", p=P),
    )

    def model_and_tiles(first, count):
        if first < MODEL_0_TILES:
            return 0, slice(first, first + count)
        return 1, slice(first - MODEL_0_TILES, first - MODEL_0_TILES + count)

    with ExitStack() as ctx:
        ctx.enter_context(tc.manual_schedule())
        const = ctx.enter_context(tc.tile_pool(name="const", bufs=1))
        scratch = ctx.enter_context(tc.tile_pool(name="scratch", bufs=4))
        small = ctx.enter_context(tc.tile_pool(name="small", bufs=3))
        y_pool = ctx.enter_context(tc.tile_pool(name="y", bufs=3))
        h_pool = ctx.enter_context(tc.tile_pool(name="h", bufs=2))
        out_pool = ctx.enter_context(tc.tile_pool(name="out", bufs=8))
        psum_t = ctx.enter_context(tc.psum_pool(name="psum_t", bufs=PAIR))
        psum_o = ctx.enter_context(tc.psum_pool(name="psum_o", bufs=OUT_BANKS))

        w_planes = const.tile([P, MODELS, N_OUT], U8, align_bytes=64)
        nc.vector.memset(w_planes[:].bitcast(I32), 0)
        eps = const.tile([P, 1], F32)
        nc.vector.memset(eps[:], EPS)
        ident = const.tile([P, P], F32)
        make_identity(nc, ident[:])
        table_warmer = const.tile([P, 1], F32)
        nc.scalar.activation(out=table_warmer[:], in_=eps[:], func=ACT.Sqrt)

        x_all = const.tile([P, TILES, H], BF16, align_bytes=4096)
        w_words = const.tile([P, MODELS, N_OUT], U32, align_bytes=4096)
        gain = const.tile([P, MODELS, PACK], BF16)

        def load_x(first, count):
            model, tiles = model_and_tiles(first, count)
            nc.sync.dma_start(out=x_all[:, first : first + count, :], in_=x_models[model][:, tiles, :])

        def load_w_words(e):
            nc.sync.dma_start(
                out=w_words[:, e, :].bitcast(I32),
                in_=W_qkv_words[e].rearrange("p n t -> p (n t)").bitcast(I32),
            )

        load_x(*X_CHUNKS_FIRST[0])
        nc.sync.dma_start(out=gain[:], in_=ln1.rearrange("e (p t) -> p e t", t=PACK))
        for r in range(SCALE_ROWS_PER_QUADRANT):
            nc.sync.dma_start(
                out=w_planes[r : P : 32, :, :].bitcast(I32),
                in_=W_qkv_scales[:, r : 16 : 4, :].rearrange("e q n -> q e n").bitcast(I32),
            )
        for first, count in X_CHUNKS_FIRST[1:]:
            load_x(first, count)
        load_w_words(0)
        for first, count in X_CHUNKS_REST:
            load_x(first, count)
        load_w_words(1)

        std_of = {}
        y_of = {}
        h_of = {}
        mx_of = {}
        result_of = {}

        def model_of(i):
            return 0 if UNITS[i][0] < MODEL_0_TILES else 1

        def stats(i):
            first, count = UNITS[i]
            sum_sq = small.tile([P, PAIR], F32)
            for jj in range(count):
                squares = scratch.tile([P, H], BF16)
                nc.scalar.activation(
                    out=squares[:], in_=x_all[:, first + jj, :], func=ACT.Square, accum_out=sum_sq[:, jj : jj + 1]
                )
            std = small.tile([P, PAIR], F32)
            nc.scalar.activation(
                out=std[:, :count], in_=sum_sq[:, :count], func=ACT.Sqrt, scale=1.0 / H, bias=eps[:, 0:1]
            )
            std_of[i] = std

        def scale(i):
            first, count = UNITS[i]
            rstd = small.tile([P, PAIR], F32)
            nc.vector.reciprocal(out=rstd[:, :count], in_=std_of[i][:, :count])
            y = y_pool.tile([P, PAIR, PACK, P], F32)
            for jj in range(count):
                nc.gpsimd.tensor_scalar(
                    out=y[:, jj, :, :],
                    in0=x_all[:, first + jj, :].rearrange("p (c t) -> p t c", t=PACK),
                    scalar1=rstd[:, jj : jj + 1],
                    scalar2=1.0,
                    op0=ALU.mult,
                    op1=ALU.mult,
                )
            y_of[i] = y

        def transpose(i):
            count = UNITS[i][1]
            h = h_pool.tile([P, PAIR, P, PACK], BF16, align_bytes=64)
            for jj in range(count):
                yT = psum_t.tile([P, PACK, P], F32)
                for t in range(PACK):
                    nc.tensor.transpose(yT[:, t, :], y_of[i][:, jj, t, :], ident[:])
                nc.vector.tensor_tensor(
                    out=h[:, jj, :, :],
                    in0=yT[:].rearrange("p t r -> p r t"),
                    in1=gain[:, model_of(i), :].unsqueeze(1).to_broadcast([P, P, PACK]),
                    op=ALU.mult,
                )
            h_of[i] = h

        def quantise(i):
            rows = UNITS[i][1] * P
            h_words = h_pool.tile([P, PAIR * P], U32, align_bytes=64)
            h_planes = h_pool.tile([P, PAIR * P], U8, align_bytes=64)
            nc.vector.quantize_mx(
                out=h_words[:, :rows].bitcast(FP8X4),
                scales=h_planes[:, :rows],
                in_=h_of[i][:, : UNITS[i][1], :, :].rearrange("p j r t -> p (j r t)"),
            )
            mx_of[i] = (h_words, h_planes)

        def multiply(i):
            e = model_of(i)
            h_words, h_planes = mx_of[i]
            first, count = UNITS[i]
            for jj in range(count):
                group, place = divmod(first + jj, PAIR)
                if place == 0:
                    result = out_pool.tile([P, PAIR, N_OUT], F32, align_bytes=4096)
                    result_of[group] = result
                rows = slice(jj * P, (jj + 1) * P)
                for block in range(BANKS_PER_TILE):
                    cols = slice(block * BANK_COLS, (block + 1) * BANK_COLS)
                    acc = psum_o.tile([P, BANK_COLS], F32)
                    nc.tensor.matmul_mx(
                        out=acc[:],
                        lhsT=h_words[:, rows].bitcast(FP8X4),
                        lhsT_scale=h_planes[:, rows],
                        rhs=w_words[:, e, cols].bitcast(FP8X4),
                        rhs_scale=w_planes[:, e, cols],
                        start=True,
                        stop=True,
                    )
                    bank = (first + jj) * BANKS_PER_TILE + block
                    if (bank % 9) % 2 == 0:
                        nc.scalar.copy(out=result_of[group][:, place, cols], in_=acc[:])
                    else:
                        nc.vector.tensor_copy(out=result_of[group][:, place, cols], in_=acc[:])
                if place == PAIR - 1:
                    model, tiles = model_and_tiles(group * PAIR, PAIR)
                    nc.sync.dma_start(out=out_models[model][:, tiles, :], in_=result_of[group][:])

        def run(stage, i):
            if 0 <= i < len(UNITS):
                stage(i)

        for step in range(len(UNITS) + 3):
            run(quantise, step - 3)
            run(stats, step)
            run(scale, step - 1)
            run(transpose, step - 2)
            run(multiply, step - 3)
